import numpy as np
import ml_dtypes


def mxq(x, axis, fmt="e4m3"):
    dtype, down = {"e4m3": (ml_dtypes.float8_e4m3fn, 7), "e5m2": (ml_dtypes.float8_e5m2, 14)}[fmt]
    v = np.moveaxis(np.asarray(x, np.float32).astype(ml_dtypes.bfloat16).astype(np.float64), axis, -1)
    blocks = v.reshape(v.shape[:-1] + (-1, 32))
    amax = np.abs(blocks).max(-1, keepdims=True)
    byte = np.maximum(np.where(amax > 0, np.frexp(amax)[1] - 1 + 127, 0) - down, 1)
    scale = np.exp2(byte - 127.0)
    codes = (blocks / scale).astype(np.float32).astype(dtype).astype(np.float64)
    return np.moveaxis((codes * scale).reshape(v.shape), -1, axis)


WIDE = False


def mx_kscale(k):
    if not WIDE:
        return np.ones(k)
    levels = np.array([10, -10, 5, -5, 0])
    if k % 512:
        return np.exp2(np.random.permutation(np.resize(levels, k // 32))).repeat(32)
    a = np.empty((k // 512, 16))
    for p in range(k // 512):
        a[p, :8] = np.random.permutation(np.resize(levels, 8))
        for g in range(8):
            far = levels[np.abs(levels - a[p, g]) >= 10]
            a[p, g + 8] = far[np.random.randint(len(far))]
    return np.exp2(a.ravel()).repeat(32)


BF16 = ml_dtypes.bfloat16


def bf(x):
    return np.asarray(x, np.float32).astype(BF16)


def f64(x):
    return np.asarray(x).astype(np.float64)


B, S, H, N, L = 2, 4096, 512, 256, 20
EPS = 1e-06
XS = np.sqrt(4.0 * EPS * L * H / N)


def setup_inputs():
    s = mx_kscale(H)
    return {"hidden_states": bf(np.random.standard_normal((B, S, H)) * XS * s),
            "conv_w": bf(np.random.standard_normal((L, N, H)) / np.sqrt(H) / s),
            "norm_w": bf(1.0 + 0.1 * np.random.standard_normal(N))}


def reference(hidden_states, conv_w, norm_w):
    x = f64(hidden_states)
    w_sum = f64(conv_w).sum(axis=0)
    out = (mxq(x, 2, "e4m3") @ mxq(w_sum, 1, "e4m3").T) / L
    sq = np.sum(out * out, axis=-1, keepdims=True)
    norm_x = np.sqrt(sq + EPS * H)
    x_normed = out / norm_x * np.sqrt(H)
    return x_normed * f64(norm_w)

@@ -1,0 +1,297 @@
+import math
+from contextlib import ExitStack
+
+import concourse.mybir as mybir
+from concourse.masks import make_identity
+
+F32 = mybir.dt.float32
+BF16 = mybir.dt.bfloat16
+U32 = mybir.dt.uint32
+U8 = mybir.dt.uint8
+FP8X4 = mybir.dt.float8_e4m3fn_x4
+ALU = mybir.AluOpType
+ACT = mybir.ActivationFunctionType
+
+P = 128
+TOKENS = 8192
+H = 512
+K = 256
+LAYERS = 20
+EPS = 1e-06
+TILES = TOKENS // P
+RT = 4
+ROUNDS = TILES // RT
+DUMMIES = 2
+
+FLOPS = 2 * TOKENS * H * K
+
+W_CHUNKS = [(0, 1), (1, 2), (2, 4), (4, 6), (6, 7), (7, 8)]
+X_CHUNKS = [(0, 4), (4, 8), (8, 12), (12, 16), (16, 24), (24, 32), (32, 40), (40, 48), (48, 56), (56, 64)]
+
+
+def tile_conv2dlinalgrmsnorm_t_kernel(tc, hidden_states, conv_w, norm_w, out):
+    nc = tc.nc
+    xv = hidden_states.flatten_outer_dims().rearrange("(p t) h -> p (t h)", t=TILES)
+    ov = out.flatten_outer_dims().rearrange("(p t) k -> p (t k)", t=TILES)
+    wv = conv_w.flatten_outer_dims().rearrange("(i p g) h -> p i g h", i=5, p=P, g=8)
+
+    with ExitStack() as ctx:
+        keep = ctx.enter_context(tc.tile_pool(name="keep", bufs=1))
+        stage = ctx.enter_context(tc.tile_pool(name="stage", bufs=3))
+        codes = ctx.enter_context(tc.tile_pool(name="codes", bufs=3))
+        psum_x = ctx.enter_context(tc.psum_pool(name="psum_x", bufs=3))
+        psum_y = ctx.enter_context(tc.psum_pool(name="psum_y", bufs=5))
+        ctx.enter_context(tc.manual_schedule())
+
+        w5 = keep.tile([P, 5, 8, H], BF16)
+        x_sb = keep.tile([P, TILES * H], BF16)
+        out_sb = keep.tile([P, TILES * K], F32)
+        ident = keep.tile([P, P], F32)
+        ident_b = keep.tile([P, P], BF16)
+        sel_f = keep.tile([P, 32], F32)
+        sel = keep.tile([P, 32], BF16)
+        ones = keep.tile([P, P], BF16)
+        nwz = keep.tile([P, K], BF16)
+        nwp = keep.tile([P, K], F32)
+        epsb = keep.tile([P, 1], F32)
+        warm = keep.tile([P, 1], F32)
+        junk = keep.tile([P, K], BF16)
+        ws1 = keep.tile([P, 2, 4, P], BF16)
+        ws3 = keep.tile([P, 2, H], BF16)
+        wg = keep.tile([P, 4 * K], BF16, align_bytes=64)
+        w_codes = keep.tile([P, K], U32, align_bytes=64)
+        w_scales = keep.tile([P, K], U8, align_bytes=64)
+
+        nc.vector.memset(nwz[:], 0.0)
+        nc.vector.memset(epsb[:], EPS * H)
+        nc.vector.memset(ones[:], 1.0)
+        first = True
+        for g0, g1 in W_CHUNKS:
+            nc.sync.dma_start(out=w5[:, :, g0:g1, :], in_=wv[:, :, g0:g1, :])
+            if first:
+                nc.sync.dma_start(out=nwz[0:1, :], in_=norm_w.unsqueeze(0))
+                first = False
+        for t0, t1 in X_CHUNKS:
+            nc.sync.dma_start(out=x_sb[:, t0 * H : t1 * H], in_=xv[:, t0 * H : t1 * H])
+        nc.scalar.activation(out=warm[:], in_=epsb[:], func=ACT.Sqrt)
+        make_identity(nc, ident[:])
+        nc.vector.tensor_reduce(
+            out=sel_f[:],
+            in_=ident[:].rearrange("p (a n) -> p n a", a=4),
+            axis=mybir.AxisListType.X,
+            op=ALU.add,
+        )
+        nc.vector.tensor_copy(out=sel[:], in_=sel_f[:])
+        nc.vector.tensor_copy(out=ident_b[:], in_=ident[:])
+
+        wt0 = psum_y.tile([P, 4, P], F32, tag="y")
+        wt1 = psum_y.tile([P, 4, P], F32, tag="y")
+        wt = [wt0, wt1]
+        s2 = psum_y.tile([P, 2, H], BF16, tag="y")
+        s4 = psum_y.tile([P, 4, 2, P], BF16, tag="y")
+        wg4 = wg[:].rearrange("p (j g t) -> p j g t", j=32, g=8, t=4)
+
+        def w_sum(g):
+            b, gl = divmod(g, 4)
+            for t in range(4):
+                for i in range(5):
+                    nc.tensor.matmul(
+                        out=wt[b][:, t, 32 * gl : 32 * gl + 32],
+                        lhsT=w5[:, i, g, P * t : P * t + P],
+                        rhs=sel[:],
+                        start=(i == 0),
+                        stop=(i == 4),
+                    )
+
+        def w_round(b):
+            nc.vector.tensor_copy(out=ws1[:, b, :, :], in_=wt[b][:])
+
+        def w_back(b):
+            for t in range(4):
+                nc.tensor.transpose(s2[:, b, P * t : P * t + P], ws1[:, b, t, :], ident_b[:])
+
+        def w_back_copy(b):
+            nc.scalar.copy(out=ws3[:, b, :], in_=s2[:, b, :])
+
+        def w_forth(b):
+            for t in range(4):
+                nc.tensor.transpose(s4[:, t, b, :], ws3[:, b, t:H:4], ident_b[:])
+
+        def w_forth_copy(b):
+            dst = wg4[:, :, 4 * b : 4 * b + 4, :]
+            src = s4[:, :, b, :].rearrange("p t (g j) -> p j g t", g=4, j=32)
+            if b == 0:
+                nc.vector.tensor_copy(out=dst, in_=src)
+            else:
+                nc.scalar.copy(out=dst, in_=src)
+
+        xw = x_sb[:].bitcast(F32)
+        xt_of = {}
+        grp_of = {}
+        code_of = {}
+        y_of = {}
+        stat_of = {}
+
+        def transposes(k, b):
+            xt = psum_x.tile([P, 2, 2, P], F32, tag="xt")
+            for a in range(2):
+                t = RT * k + 2 * b + a
+                for u in range(2):
+                    c0 = 256 * t + u
+                    nc.tensor.transpose(xt[:, a, u, :], xw[:, c0 : 256 * (t + 1) : 2], ident[:])
+            xt_of[(k, b)] = xt
+
+        def copy_out(k, b, on_vector):
+            if b == 0:
+                grp = stage.tile([P, RT * H], BF16, align_bytes=64, tag="grp")
+                grp_of[k] = grp
+            g32 = grp_of[k][:].bitcast(F32)
+            dst = g32[:, 512 * b : 512 * b + 512].rearrange("p (a r u) -> p a r u", a=2, r=P, u=2)
+            src = xt_of[(k, b)][:].rearrange("p a u r -> p a r u")
+            if on_vector:
+                nc.vector.tensor_copy(out=dst, in_=src)
+            else:
+                nc.scalar.copy(out=dst, in_=src)
+
+        def quantise(k):
+            xc = codes.tile([P, RT * P], U32, align_bytes=64, tag="xc")
+            xs = codes.tile([P, RT * P], U8, align_bytes=64, tag="xs")
+            nc.vector.quantize_mx(out=xc[:].bitcast(FP8X4), scales=xs[:], in_=grp_of[k][:])
+            code_of[k] = (xc, xs)
+
+        def passes(k):
+            xc, xs = code_of[k]
+            banks = []
+            for b in range(2):
+                y = psum_y.tile([P, 2, K], F32, tag="y")
+                if k > 0 and b < DUMMIES:
+                    nc.tensor.matmul_mx(
+                        out=y[:].rearrange("p a k -> p (a k)"),
+                        lhsT=xc[:, 0:P].bitcast(FP8X4),
+                        lhsT_scale=xs[:, 0:P],
+                        rhs=xc[:].bitcast(FP8X4),
+                        rhs_scale=xs[:],
+                        start=True,
+                        stop=True,
+                    )
+                for a in range(2):
+                    c0 = P * (2 * b + a)
+                    nc.tensor.matmul_mx(
+                        out=y[:, a, :],
+                        lhsT=xc[:, c0 : c0 + P].bitcast(FP8X4),
+                        lhsT_scale=xs[:, c0 : c0 + P],
+                        rhs=w_codes[:].bitcast(FP8X4),
+                        rhs_scale=w_scales[:],
+                        start=True,
+                        stop=True,
+                    )
+                banks.append(y)
+            y_of[k] = banks
+
+        def squares(k):
+            q = stage.tile([P, RT], F32, tag="q")
+            n = stage.tile([P, RT], F32, tag="n")
+            for j0, j1 in cuts(k):
+                for j in range(j0, j1):
+                    nc.scalar.activation(
+                        out=junk[:],
+                        in_=y_of[k][j // 2][:, j % 2, :],
+                        func=ACT.Square,
+                        accum_out=q[:, j : j + 1],
+                    )
+                nc.scalar.activation(
+                    out=n[:, j0:j1],
+                    in_=q[:, j0:j1],
+                    func=ACT.Sqrt,
+                    bias=epsb[:],
+                    scale=1.0 / (LAYERS * LAYERS),
+                )
+            r = stage.tile([P, RT], F32, tag="r")
+            stat_of[k] = (n, r)
+
+        def reciprocal(k, j0, j1):
+            n, r = stat_of[k]
+            nc.vector.reciprocal(out=r[:, j0:j1], in_=n[:, j0:j1])
+
+        def final(k, j0, j1):
+            r = stat_of[k][1]
+            for j in range(j0, j1):
+                t = RT * k + j
+                nc.vector.scalar_tensor_tensor(
+                    out=out_sb[:, t * K : (t + 1) * K],
+                    in0=y_of[k][j // 2][:, j % 2, :],
+                    scalar=r[:, j : j + 1],
+                    in1=nwp[:],
+                    op0=ALU.mult,
+                    op1=ALU.mult,
+                )
+
+        def store(k, j0, j1):
+            c0 = (RT * k + j0) * K
+            c1 = (RT * k + j1) * K
+            nc.sync.dma_start(out=ov[:, c0:c1], in_=out_sb[:, c0:c1])
+
+        def cuts(k):
+            if k == ROUNDS - 1:
+                return [(0, 2), (2, 3), (3, 4)]
+            return [(0, RT)]
+
+        def on_vector(k, b):
+            return b == 1
+
+        w_sum(0)
+        nw_ps = psum_x.tile([P, K], F32, tag="xt")
+        nc.tensor.matmul(out=nw_ps[:], lhsT=ones[:], rhs=nwz[:], start=True, stop=True)
+        nc.vector.tensor_scalar_mul(out=nwp[:], in0=nw_ps[:], scalar1=math.sqrt(H) / LAYERS)
+        w_sum(1)
+        w_sum(2)
+        w_sum(3)
+        w_round(0)
+        w_sum(4)
+        w_back(0)
+        w_back_copy(0)
+        w_sum(5)
+        w_forth(0)
+        w_forth_copy(0)
+        w_sum(6)
+        w_sum(7)
+        w_round(1)
+        transposes(0, 0)
+        w_back(1)
+        copy_out(0, 0, False)
+        w_back_copy(1)
+        transposes(0, 1)
+        w_forth(1)
+        copy_out(0, 1, True)
+        quantise(0)
+        w_forth_copy(1)
+        nc.vector.quantize_mx(out=w_codes[:].bitcast(FP8X4), scales=w_scales[:], in_=wg[:])
+        transposes(1, 0)
+        transposes(1, 1)
+        copy_out(1, 0, False)
+        copy_out(1, 1, True)
+        passes(0)
+
+        for k in range(ROUNDS + 1):
+            a = k + 2
+            if a < ROUNDS:
+                transposes(a, 0)
+                transposes(a, 1)
+            if 1 <= k < ROUNDS:
+                reciprocal(k - 1, 0, RT)
+                final(k - 1, 0, 1)
+            if k + 1 < ROUNDS:
+                quantise(k + 1)
+                passes(k + 1)
+            if 1 <= k < ROUNDS:
+                final(k - 1, 1, RT)
+                store(k - 1, 0, RT)
+            if k < ROUNDS:
+                squares(k)
+            if a < ROUNDS:
+                copy_out(a, 0, on_vector(a, 0))
+                copy_out(a, 1, on_vector(a, 1))
+        for j0, j1 in cuts(ROUNDS - 1):
+            reciprocal(ROUNDS - 1, j0, j1)
+            final(ROUNDS - 1, j0, j1)
+            store(ROUNDS - 1, j0, j1)

@@ -23,9 +23,12 @@ RT = 4
 ROUNDS = TILES // RT
 DUMMIES = 2
 
+PAD = 32
+
 FLOPS = 2 * TOKENS * H * K
 
 W_CHUNKS = [(0, 1), (1, 2), (2, 4), (4, 6), (6, 7), (7, 8)]
+W_BANKS = [(0, 4), (4, 7), (7, 8)]
 X_CHUNKS = [(0, 4), (4, 8), (8, 12), (12, 16), (16, 24), (24, 32), (32, 40), (40, 48), (48, 56), (56, 64)]
 
 
@@ -38,16 +41,21 @@ def tile_conv2dlinalgrmsnorm_t_kernel(tc, hidden_states, conv_w, norm_w, out):
     with ExitStack() as ctx:
         keep = ctx.enter_context(tc.tile_pool(name="keep", bufs=1))
         stage = ctx.enter_context(tc.tile_pool(name="stage", bufs=3))
-        codes = ctx.enter_context(tc.tile_pool(name="codes", bufs=3))
+        codes = ctx.enter_context(tc.tile_pool(name="codes", bufs=4))
         psum_x = ctx.enter_context(tc.psum_pool(name="psum_x", bufs=3))
         psum_y = ctx.enter_context(tc.psum_pool(name="psum_y", bufs=5))
         ctx.enter_context(tc.manual_schedule())
 
-        w5 = keep.tile([P, 5, 8, H], BF16)
-        x_sb = keep.tile([P, TILES * H], BF16)
+        w_tiles = []
+        for c, (g0, g1) in enumerate(W_CHUNKS):
+            wc = keep.tile([P, 5 * (g1 - g0) * H + PAD], BF16, name=f"wc{c}")
+            w_tiles.append(wc)
+        x_tiles = []
+        for c, (t0, t1) in enumerate(X_CHUNKS):
+            xc = keep.tile([P, (t1 - t0) * H + PAD], BF16, name=f"xc{c}")
+            x_tiles.append(xc)
         out_sb = keep.tile([P, TILES * K], F32)
         ident = keep.tile([P, P], F32)
-        ident_b = keep.tile([P, P], BF16)
         sel_f = keep.tile([P, 32], F32)
         sel = keep.tile([P, 32], BF16)
         ones = keep.tile([P, P], BF16)
@@ -56,8 +64,6 @@ def tile_conv2dlinalgrmsnorm_t_kernel(tc, hidden_states, conv_w, norm_w, out):
         epsb = keep.tile([P, 1], F32)
         warm = keep.tile([P, 1], F32)
         junk = keep.tile([P, K], BF16)
-        ws1 = keep.tile([P, 2, 4, P], BF16)
-        ws3 = keep.tile([P, 2, H], BF16)
         wg = keep.tile([P, 4 * K], BF16, align_bytes=64)
         w_codes = keep.tile([P, K], U32, align_bytes=64)
         w_scales = keep.tile([P, K], U8, align_bytes=64)
@@ -66,13 +72,19 @@ def tile_conv2dlinalgrmsnorm_t_kernel(tc, hidden_states, conv_w, norm_w, out):
         nc.vector.memset(epsb[:], EPS * H)
         nc.vector.memset(ones[:], 1.0)
         first = True
-        for g0, g1 in W_CHUNKS:
-            nc.sync.dma_start(out=w5[:, :, g0:g1, :], in_=wv[:, :, g0:g1, :])
+        for c, (g0, g1) in enumerate(W_CHUNKS):
+            n = g1 - g0
+            nc.sync.dma_start(
+                out=w_tiles[c][:, 0 : 5 * n * H].rearrange("p (i g h) -> p i g h", i=5, g=n),
+                in_=wv[:, :, g0:g1, :],
+            )
             if first:
                 nc.sync.dma_start(out=nwz[0:1, :], in_=norm_w.unsqueeze(0))
                 first = False
-        for t0, t1 in X_CHUNKS:
-            nc.sync.dma_start(out=x_sb[:, t0 * H : t1 * H], in_=xv[:, t0 * H : t1 * H])
+        for c, (t0, t1) in enumerate(X_CHUNKS):
+            nc.sync.dma_start(
+                out=x_tiles[c][:, 0 : (t1 - t0) * H], in_=xv[:, t0 * H : t1 * H]
+            )
         nc.scalar.activation(out=warm[:], in_=epsb[:], func=ACT.Sqrt)
         make_identity(nc, ident[:])
         nc.vector.tensor_reduce(
@@ -82,50 +94,37 @@ def tile_conv2dlinalgrmsnorm_t_kernel(tc, hidden_states, conv_w, norm_w, out):
             op=ALU.add,
         )
         nc.vector.tensor_copy(out=sel[:], in_=sel_f[:])
-        nc.vector.tensor_copy(out=ident_b[:], in_=ident[:])
 
-        wt0 = psum_y.tile([P, 4, P], F32, tag="y")
-        wt1 = psum_y.tile([P, 4, P], F32, tag="y")
-        wt = [wt0, wt1]
-        s2 = psum_y.tile([P, 2, H], BF16, tag="y")
-        s4 = psum_y.tile([P, 4, 2, P], BF16, tag="y")
         wg4 = wg[:].rearrange("p (j g t) -> p j g t", j=32, g=8, t=4)
+        wt_of = {}
 
         def w_sum(g):
-            b, gl = divmod(g, 4)
+            b = [i for i, (g0, g1) in enumerate(W_BANKS) if g0 <= g < g1][0]
+            g0 = W_BANKS[b][0]
+            if g == g0:
+                wt = psum_y.tile([P, 4, P], F32, tag="y")
+                wt_of[b] = wt
+            c = [i for i, (c0, c1) in enumerate(W_CHUNKS) if c0 <= g < c1][0]
+            c0, c1 = W_CHUNKS[c]
             for t in range(4):
                 for i in range(5):
+                    h0 = (i * (c1 - c0) + g - c0) * H
                     nc.tensor.matmul(
-                        out=wt[b][:, t, 32 * gl : 32 * gl + 32],
-                        lhsT=w5[:, i, g, P * t : P * t + P],
+                        out=wt_of[b][:, t, 32 * (g - g0) : 32 * (g - g0) + 32],
+                        lhsT=w_tiles[c][:, h0 + t : h0 + H : 4],
                         rhs=sel[:],
                         start=(i == 0),
                         stop=(i == 4),
                     )
 
         def w_round(b):
-            nc.vector.tensor_copy(out=ws1[:, b, :, :], in_=wt[b][:])
+            g0, g1 = W_BANKS[b]
+            n = g1 - g0
+            nc.vector.tensor_copy(
+                out=wg4[:, :, g0:g1, :],
+                in_=wt_of[b][:, :, 0 : 32 * n].rearrange("p t (g j) -> p j g t", g=n, j=32),
+            )
 
-        def w_back(b):
-            for t in range(4):
-                nc.tensor.transpose(s2[:, b, P * t : P * t + P], ws1[:, b, t, :], ident_b[:])
-
-        def w_back_copy(b):
-            nc.scalar.copy(out=ws3[:, b, :], in_=s2[:, b, :])
-
-        def w_forth(b):
-            for t in range(4):
-                nc.tensor.transpose(s4[:, t, b, :], ws3[:, b, t:H:4], ident_b[:])
-
-        def w_forth_copy(b):
-            dst = wg4[:, :, 4 * b : 4 * b + 4, :]
-            src = s4[:, :, b, :].rearrange("p t (g j) -> p j g t", g=4, j=32)
-            if b == 0:
-                nc.vector.tensor_copy(out=dst, in_=src)
-            else:
-                nc.scalar.copy(out=dst, in_=src)
-
-        xw = x_sb[:].bitcast(F32)
         xt_of = {}
         grp_of = {}
         code_of = {}
@@ -136,9 +135,11 @@ def tile_conv2dlinalgrmsnorm_t_kernel(tc, hidden_states, conv_w, norm_w, out):
             xt = psum_x.tile([P, 2, 2, P], F32, tag="xt")
             for a in range(2):
                 t = RT * k + 2 * b + a
+                c = [i for i, (t0, t1) in enumerate(X_CHUNKS) if t0 <= t < t1][0]
+                xw = x_tiles[c][:].bitcast(F32)
+                c0 = 256 * (t - X_CHUNKS[c][0])
                 for u in range(2):
-                    c0 = 256 * t + u
-                    nc.tensor.transpose(xt[:, a, u, :], xw[:, c0 : 256 * (t + 1) : 2], ident[:])
+                    nc.tensor.transpose(xt[:, a, u, :], xw[:, c0 + u : c0 + 256 : 2], ident[:])
             xt_of[(k, b)] = xt
 
         def copy_out(k, b, on_vector):
@@ -243,49 +244,39 @@ def tile_conv2dlinalgrmsnorm_t_kernel(tc, hidden_states, conv_w, norm_w, out):
         nw_ps = psum_x.tile([P, K], F32, tag="xt")
         nc.tensor.matmul(out=nw_ps[:], lhsT=ones[:], rhs=nwz[:], start=True, stop=True)
         nc.vector.tensor_scalar_mul(out=nwp[:], in0=nw_ps[:], scalar1=math.sqrt(H) / LAYERS)
-        w_sum(1)
-        w_sum(2)
-        w_sum(3)
-        w_round(0)
-        w_sum(4)
-        w_back(0)
-        w_back_copy(0)
-        w_sum(5)
-        w_forth(0)
-        w_forth_copy(0)
-        w_sum(6)
-        w_sum(7)
+        for g in range(1, 7):
+            w_sum(g)
+            if g == 4:
+                w_round(0)
         w_round(1)
-        transposes(0, 0)
-        w_back(1)
-        copy_out(0, 0, False)
-        w_back_copy(1)
-        transposes(0, 1)
-        w_forth(1)
-        copy_out(0, 1, True)
-        quantise(0)
-        w_forth_copy(1)
+        w_sum(7)
+        w_round(2)
         nc.vector.quantize_mx(out=w_codes[:].bitcast(FP8X4), scales=w_scales[:], in_=wg[:])
-        transposes(1, 0)
-        transposes(1, 1)
-        copy_out(1, 0, False)
-        copy_out(1, 1, True)
+        for k in range(2):
+            transposes(k, 0)
+            transposes(k, 1)
+            copy_out(k, 0, on_vector(k, 0))
+            copy_out(k, 1, on_vector(k, 1))
+            quantise(k)
         passes(0)
+        transposes(2, 0)
+        transposes(2, 1)
+        copy_out(2, 0, on_vector(2, 0))
+        copy_out(2, 1, on_vector(2, 1))
 
         for k in range(ROUNDS + 1):
-            a = k + 2
+            a = k + 3
             if a < ROUNDS:
                 transposes(a, 0)
                 transposes(a, 1)
             if 1 <= k < ROUNDS:
                 reciprocal(k - 1, 0, RT)
-                final(k - 1, 0, 1)
-            if k + 1 < ROUNDS:
-                quantise(k + 1)
-                passes(k + 1)
-            if 1 <= k < ROUNDS:
-                final(k - 1, 1, RT)
+                final(k - 1, 0, RT)
                 store(k - 1, 0, RT)
+            if k + 2 < ROUNDS:
+                quantise(k + 2)
+            if k + 1 < ROUNDS:
+                passes(k + 1)
             if k < ROUNDS:
                 squares(k)
             if a < ROUNDS:

@@ -27,9 +27,9 @@ PAD = 32
 
 FLOPS = 2 * TOKENS * H * K
 
-W_CHUNKS = [(0, 1), (1, 2), (2, 4), (4, 6), (6, 7), (7, 8)]
-W_BANKS = [(0, 4), (4, 7), (7, 8)]
-X_CHUNKS = [(0, 4), (4, 8), (8, 12), (12, 16), (16, 24), (24, 32), (32, 40), (40, 48), (48, 56), (56, 64)]
+W_CHUNKS = [(0, 4), (4, 8)]
+W_BANKS = [(0, 4), (4, 8)]
+X_CHUNKS = [(0, 4), (4, 8), (8, 16), (16, 24), (24, 32), (32, 40), (40, 48), (48, 56), (56, 64)]
 
 
 def tile_conv2dlinalgrmsnorm_t_kernel(tc, hidden_states, conv_w, norm_w, out):
@@ -248,9 +248,8 @@ def tile_conv2dlinalgrmsnorm_t_kernel(tc, hidden_states, conv_w, norm_w, out):
             w_sum(g)
             if g == 4:
                 w_round(0)
-        w_round(1)
         w_sum(7)
-        w_round(2)
+        w_round(1)
         nc.vector.quantize_mx(out=w_codes[:].bitcast(FP8X4), scales=w_scales[:], in_=wg[:])
         for k in range(2):
             transposes(k, 0)
@@ -272,7 +271,10 @@ def tile_conv2dlinalgrmsnorm_t_kernel(tc, hidden_states, conv_w, norm_w, out):
             if 1 <= k < ROUNDS:
                 reciprocal(k - 1, 0, RT)
                 final(k - 1, 0, RT)
-                store(k - 1, 0, RT)
+                if k - 1 >= ROUNDS - 2:
+                    store(k - 1, 0, RT)
+                elif (k - 1) % 2 == 1:
+                    store(k - 2, 0, 2 * RT)
             if k + 2 < ROUNDS:
                 quantise(k + 2)
             if k + 1 < ROUNDS:

@@ -21,7 +21,6 @@ EPS = 1e-06
 TILES = TOKENS // P
 RT = 4
 ROUNDS = TILES // RT
-DUMMIES = 2
 
 PAD = 32
 
@@ -165,16 +164,6 @@ def tile_conv2dlinalgrmsnorm_t_kernel(tc, hidden_states, conv_w, norm_w, out):
             banks = []
             for b in range(2):
                 y = psum_y.tile([P, 2, K], F32, tag="y")
-                if k > 0 and b < DUMMIES:
-                    nc.tensor.matmul_mx(
-                        out=y[:].rearrange("p a k -> p (a k)"),
-                        lhsT=xc[:, 0:P].bitcast(FP8X4),
-                        lhsT_scale=xs[:, 0:P],
-                        rhs=xc[:].bitcast(FP8X4),
-                        rhs_scale=xs[:],
-                        start=True,
-                        stop=True,
-                    )
                 for a in range(2):
                     c0 = P * (2 * b + a)
                     nc.tensor.matmul_mx(

@@ -19,6 +19,7 @@ K = 256
 LAYERS = 20
 EPS = 1e-06
 TILES = TOKENS // P
+CT = 8
 RT = 4
 ROUNDS = TILES // RT
 
@@ -33,8 +34,8 @@ X_CHUNKS = [(0, 4), (4, 8), (8, 16), (16, 24), (24, 32), (32, 40), (40, 48), (48
 
 def tile_conv2dlinalgrmsnorm_t_kernel(tc, hidden_states, conv_w, norm_w, out):
     nc = tc.nc
-    xv = hidden_states.flatten_outer_dims().rearrange("(p t) h -> p (t h)", t=TILES)
-    ov = out.flatten_outer_dims().rearrange("(p t) k -> p (t k)", t=TILES)
+    xv = hidden_states.flatten_outer_dims().rearrange("(n p t) h -> n p (t h)", p=P, t=CT)
+    ov = out.flatten_outer_dims().rearrange("(n p t) k -> n p (t k)", p=P, t=CT)
     wv = conv_w.flatten_outer_dims().rearrange("(i p g) h -> p i g h", i=5, p=P, g=8)
 
     with ExitStack() as ctx:
@@ -82,7 +83,7 @@ def tile_conv2dlinalgrmsnorm_t_kernel(tc, hidden_states, conv_w, norm_w, out):
                 first = False
         for c, (t0, t1) in enumerate(X_CHUNKS):
             nc.sync.dma_start(
-                out=x_tiles[c][:, 0 : (t1 - t0) * H], in_=xv[:, t0 * H : t1 * H]
+                out=x_tiles[c][:, 0 : (t1 - t0) * H], in_=xv[t0 // CT][:, t0 % CT * H : (t0 % CT + t1 - t0) * H]
             )
         nc.scalar.activation(out=warm[:], in_=epsb[:], func=ACT.Sqrt)
         make_identity(nc, ident[:])
@@ -217,9 +218,12 @@ def tile_conv2dlinalgrmsnorm_t_kernel(tc, hidden_states, conv_w, norm_w, out):
                 )
 
         def store(k, j0, j1):
-            c0 = (RT * k + j0) * K
-            c1 = (RT * k + j1) * K
-            nc.sync.dma_start(out=ov[:, c0:c1], in_=out_sb[:, c0:c1])
+            t0 = RT * k + j0
+            t1 = RT * k + j1
+            n, u0 = divmod(t0, CT)
+            nc.sync.dma_start(
+                out=ov[n][:, u0 * K : (u0 + t1 - t0) * K], in_=out_sb[:, t0 * K : t1 * K]
+            )
 
         def cuts(k):
             if k == ROUNDS - 1:

@@ -85,7 +85,7 @@ def tile_conv2dlinalgrmsnorm_t_kernel(tc, hidden_states, conv_w, norm_w, out):
             nc.sync.dma_start(
                 out=x_tiles[c][:, 0 : (t1 - t0) * H], in_=xv[t0 // CT][:, t0 % CT * H : (t0 % CT + t1 - t0) * H]
             )
-        nc.scalar.activation(out=warm[:], in_=epsb[:], func=ACT.Sqrt)
+        nc.scalar.activation(out=warm[:], in_=epsb[:], func=ACT.Abs_reciprocal_sqrt)
         make_identity(nc, ident[:])
         nc.vector.tensor_reduce(
             out=sel_f[:],
@@ -179,30 +179,29 @@ def tile_conv2dlinalgrmsnorm_t_kernel(tc, hidden_states, conv_w, norm_w, out):
                 banks.append(y)
             y_of[k] = banks
 
-        def squares(k):
-            q = stage.tile([P, RT], F32, tag="q")
-            n = stage.tile([P, RT], F32, tag="n")
-            for j0, j1 in cuts(k):
-                for j in range(j0, j1):
-                    nc.scalar.activation(
-                        out=junk[:],
-                        in_=y_of[k][j // 2][:, j % 2, :],
-                        func=ACT.Square,
-                        accum_out=q[:, j : j + 1],
-                    )
+        def squares(k, j0, j1):
+            if j0 == 0:
+                q = stage.tile([P, RT], F32, tag="q")
+                r = stage.tile([P, RT], F32, tag="r")
+                stat_of[k] = (q, r)
+            q = stat_of[k][0]
+            for j in range(j0, j1):
                 nc.scalar.activation(
-                    out=n[:, j0:j1],
-                    in_=q[:, j0:j1],
-                    func=ACT.Sqrt,
-                    bias=epsb[:],
-                    scale=1.0 / (LAYERS * LAYERS),
+                    out=junk[:],
+                    in_=y_of[k][j // 2][:, j % 2, :],
+                    func=ACT.Square,
+                    accum_out=q[:, j : j + 1],
                 )
-            r = stage.tile([P, RT], F32, tag="r")
-            stat_of[k] = (n, r)
 
-        def reciprocal(k, j0, j1):
-            n, r = stat_of[k]
-            nc.vector.reciprocal(out=r[:, j0:j1], in_=n[:, j0:j1])
+        def rstd(k, j0, j1):
+            q, r = stat_of[k]
+            nc.scalar.activation(
+                out=r[:, j0:j1],
+                in_=q[:, j0:j1],
+                func=ACT.Abs_reciprocal_sqrt,
+                bias=epsb[:],
+                scale=1.0 / (LAYERS * LAYERS),
+            )
 
         def final(k, j0, j1):
             r = stat_of[k][1]
@@ -256,28 +255,31 @@ def tile_conv2dlinalgrmsnorm_t_kernel(tc, hidden_states, conv_w, norm_w, out):
         copy_out(2, 0, on_vector(2, 0))
         copy_out(2, 1, on_vector(2, 1))
 
-        for k in range(ROUNDS + 1):
+        last = ROUNDS - 1
+        for k in range(ROUNDS):
             a = k + 3
             if a < ROUNDS:
                 transposes(a, 0)
                 transposes(a, 1)
-            if 1 <= k < ROUNDS:
-                reciprocal(k - 1, 0, RT)
+            if k >= 1:
                 final(k - 1, 0, RT)
                 if k - 1 >= ROUNDS - 2:
                     store(k - 1, 0, RT)
                 elif (k - 1) % 2 == 1:
                     store(k - 2, 0, 2 * RT)
-            if k + 2 < ROUNDS:
-                quantise(k + 2)
             if k + 1 < ROUNDS:
                 passes(k + 1)
-            if k < ROUNDS:
-                squares(k)
+            if k < last:
+                squares(k, 0, RT)
             if a < ROUNDS:
                 copy_out(a, 0, on_vector(a, 0))
                 copy_out(a, 1, on_vector(a, 1))
-        for j0, j1 in cuts(ROUNDS - 1):
-            reciprocal(ROUNDS - 1, j0, j1)
-            final(ROUNDS - 1, j0, j1)
-            store(ROUNDS - 1, j0, j1)
+            if k + 2 < ROUNDS:
+                quantise(k + 2)
+            if k < last:
+                rstd(k, 0, RT)
+        for j0, j1 in cuts(last):
+            squares(last, j0, j1)
+            rstd(last, j0, j1)
+            final(last, j0, j1)
+            store(last, j0, j1)

@@ -27,8 +27,7 @@ PAD = 32
 
 FLOPS = 2 * TOKENS * H * K
 
-W_CHUNKS = [(0, 4), (4, 8)]
-W_BANKS = [(0, 4), (4, 8)]
+W_CHUNKS = [(0, 2), (2, 4), (4, 6), (6, 7), (7, 8)]
 X_CHUNKS = [(0, 4), (4, 8), (8, 16), (16, 24), (24, 32), (32, 40), (40, 48), (48, 56), (56, 64)]
 
 
@@ -71,20 +70,30 @@ def tile_conv2dlinalgrmsnorm_t_kernel(tc, hidden_states, conv_w, norm_w, out):
         nc.vector.memset(nwz[:], 0.0)
         nc.vector.memset(epsb[:], EPS * H)
         nc.vector.memset(ones[:], 1.0)
-        first = True
-        for c, (g0, g1) in enumerate(W_CHUNKS):
+        def load_w(c):
+            g0, g1 = W_CHUNKS[c]
             n = g1 - g0
             nc.sync.dma_start(
                 out=w_tiles[c][:, 0 : 5 * n * H].rearrange("p (i g h) -> p i g h", i=5, g=n),
                 in_=wv[:, :, g0:g1, :],
             )
-            if first:
-                nc.sync.dma_start(out=nwz[0:1, :], in_=norm_w.unsqueeze(0))
-                first = False
-        for c, (t0, t1) in enumerate(X_CHUNKS):
+
+        def load_x(c):
+            t0, t1 = X_CHUNKS[c]
+            n, u0 = divmod(t0, CT)
             nc.sync.dma_start(
-                out=x_tiles[c][:, 0 : (t1 - t0) * H], in_=xv[t0 // CT][:, t0 % CT * H : (t0 % CT + t1 - t0) * H]
+                out=x_tiles[c][:, 0 : (t1 - t0) * H],
+                in_=xv[n][:, u0 * H : (u0 + t1 - t0) * H],
             )
+
+        load_w(0)
+        nc.sync.dma_start(out=nwz[0:1, :], in_=norm_w.unsqueeze(0))
+        for c in range(1, 4):
+            load_w(c)
+        load_x(0)
+        load_w(4)
+        for c in range(1, len(X_CHUNKS)):
+            load_x(c)
         nc.scalar.activation(out=warm[:], in_=epsb[:], func=ACT.Abs_reciprocal_sqrt)
         make_identity(nc, ident[:])
         nc.vector.tensor_reduce(
@@ -98,31 +107,28 @@ def tile_conv2dlinalgrmsnorm_t_kernel(tc, hidden_states, conv_w, norm_w, out):
         wg4 = wg[:].rearrange("p (j g t) -> p j g t", j=32, g=8, t=4)
         wt_of = {}
 
-        def w_sum(g):
-            b = [i for i, (g0, g1) in enumerate(W_BANKS) if g0 <= g < g1][0]
-            g0 = W_BANKS[b][0]
-            if g == g0:
-                wt = psum_y.tile([P, 4, P], F32, tag="y")
-                wt_of[b] = wt
-            c = [i for i, (c0, c1) in enumerate(W_CHUNKS) if c0 <= g < c1][0]
-            c0, c1 = W_CHUNKS[c]
-            for t in range(4):
-                for i in range(5):
-                    h0 = (i * (c1 - c0) + g - c0) * H
-                    nc.tensor.matmul(
-                        out=wt_of[b][:, t, 32 * (g - g0) : 32 * (g - g0) + 32],
-                        lhsT=w_tiles[c][:, h0 + t : h0 + H : 4],
-                        rhs=sel[:],
-                        start=(i == 0),
-                        stop=(i == 4),
-                    )
-
-        def w_round(b):
-            g0, g1 = W_BANKS[b]
+        def w_sum(c):
+            g0, g1 = W_CHUNKS[c]
             n = g1 - g0
+            wt = psum_y.tile([P, 4, 32 * n], F32, tag="y")
+            wt_of[c] = wt
+            for g in range(n):
+                for t in range(4):
+                    for i in range(5):
+                        h0 = (i * n + g) * H
+                        nc.tensor.matmul(
+                            out=wt[:, t, 32 * g : 32 * g + 32],
+                            lhsT=w_tiles[c][:, h0 + t : h0 + H : 4],
+                            rhs=sel[:],
+                            start=(i == 0),
+                            stop=(i == 4),
+                        )
+
+        def w_round(c):
+            g0, g1 = W_CHUNKS[c]
             nc.vector.tensor_copy(
                 out=wg4[:, :, g0:g1, :],
-                in_=wt_of[b][:, :, 0 : 32 * n].rearrange("p t (g j) -> p j g t", g=n, j=32),
+                in_=wt_of[c][:].rearrange("p t (g j) -> p j g t", g=g1 - g0, j=32),
             )
 
         xt_of = {}
@@ -224,36 +230,32 @@ def tile_conv2dlinalgrmsnorm_t_kernel(tc, hidden_states, conv_w, norm_w, out):
                 out=ov[n][:, u0 * K : (u0 + t1 - t0) * K], in_=out_sb[:, t0 * K : t1 * K]
             )
 
-        def cuts(k):
-            if k == ROUNDS - 1:
-                return [(0, 2), (2, 3), (3, 4)]
-            return [(0, RT)]
-
         def on_vector(k, b):
             return b == 1
+
+        def prepare(k):
+            for b in range(2):
+                transposes(k, b)
+            for b in range(2):
+                copy_out(k, b, on_vector(k, b))
 
         w_sum(0)
         nw_ps = psum_x.tile([P, K], F32, tag="xt")
         nc.tensor.matmul(out=nw_ps[:], lhsT=ones[:], rhs=nwz[:], start=True, stop=True)
         nc.vector.tensor_scalar_mul(out=nwp[:], in0=nw_ps[:], scalar1=math.sqrt(H) / LAYERS)
-        for g in range(1, 7):
-            w_sum(g)
-            if g == 4:
-                w_round(0)
-        w_sum(7)
-        w_round(1)
+        w_round(0)
+        for c in range(1, 4):
+            w_sum(c)
+            w_round(c)
+        prepare(0)
+        quantise(0)
+        w_sum(4)
+        w_round(4)
         nc.vector.quantize_mx(out=w_codes[:].bitcast(FP8X4), scales=w_scales[:], in_=wg[:])
-        for k in range(2):
-            transposes(k, 0)
-            transposes(k, 1)
-            copy_out(k, 0, on_vector(k, 0))
-            copy_out(k, 1, on_vector(k, 1))
-            quantise(k)
+        prepare(1)
         passes(0)
-        transposes(2, 0)
-        transposes(2, 1)
-        copy_out(2, 0, on_vector(2, 0))
-        copy_out(2, 1, on_vector(2, 1))
+        quantise(1)
+        prepare(2)
 
         last = ROUNDS - 1
         for k in range(ROUNDS):
@@ -278,8 +280,9 @@ def tile_conv2dlinalgrmsnorm_t_kernel(tc, hidden_states, conv_w, norm_w, out):
                 quantise(k + 2)
             if k < last:
                 rstd(k, 0, RT)
-        for j0, j1 in cuts(last):
+        for j0, j1 in [(0, 2), (2, 4)]:
             squares(last, j0, j1)
             rstd(last, j0, j1)
-            final(last, j0, j1)
-            store(last, j0, j1)
+            for j in range(j0, j1):
+                final(last, j, j + 1)
+                store(last, j, j + 1)

@@ -231,7 +231,7 @@ def tile_conv2dlinalgrmsnorm_t_kernel(tc, hidden_states, conv_w, norm_w, out):
             )
 
         def on_vector(k, b):
-            return b == 1
+            return b == 1 or k % 4 == 3
 
         def prepare(k):
             for b in range(2):

@@ -28,7 +28,7 @@ PAD = 32
 FLOPS = 2 * TOKENS * H * K
 
 W_CHUNKS = [(0, 2), (2, 4), (4, 6), (6, 7), (7, 8)]
-X_CHUNKS = [(0, 4), (4, 8), (8, 16), (16, 24), (24, 32), (32, 40), (40, 48), (48, 56), (56, 64)]
+X_CHUNKS = [(0, 4), (4, 8), (8, 12), (12, 16), (16, 24), (24, 32), (32, 40), (40, 48), (48, 56), (56, 64)]
 
 
 def tile_conv2dlinalgrmsnorm_t_kernel(tc, hidden_states, conv_w, norm_w, out):
@@ -88,9 +88,10 @@ def tile_conv2dlinalgrmsnorm_t_kernel(tc, hidden_states, conv_w, norm_w, out):
 
         load_w(0)
         nc.sync.dma_start(out=nwz[0:1, :], in_=norm_w.unsqueeze(0))
-        for c in range(1, 4):
-            load_w(c)
+        load_w(1)
+        load_w(2)
         load_x(0)
+        load_w(3)
         load_w(4)
         for c in range(1, len(X_CHUNKS)):
             load_x(c)
@@ -231,7 +232,7 @@ def tile_conv2dlinalgrmsnorm_t_kernel(tc, hidden_states, conv_w, norm_w, out):
             )
 
         def on_vector(k, b):
-            return b == 1 or k % 4 == 3
+            return b == 1 or k % 5 == 4
 
         def prepare(k):
             for b in range(2):
@@ -244,17 +245,20 @@ def tile_conv2dlinalgrmsnorm_t_kernel(tc, hidden_states, conv_w, norm_w, out):
         nc.tensor.matmul(out=nw_ps[:], lhsT=ones[:], rhs=nwz[:], start=True, stop=True)
         nc.vector.tensor_scalar_mul(out=nwp[:], in0=nw_ps[:], scalar1=math.sqrt(H) / LAYERS)
         w_round(0)
-        for c in range(1, 4):
-            w_sum(c)
-            w_round(c)
+        w_sum(1)
+        w_round(1)
+        w_sum(2)
+        w_round(2)
         prepare(0)
+        w_sum(3)
+        w_round(3)
         quantise(0)
         w_sum(4)
         w_round(4)
         nc.vector.quantize_mx(out=w_codes[:].bitcast(FP8X4), scales=w_scales[:], in_=wg[:])
         prepare(1)
-        passes(0)
         quantise(1)
+        passes(0)
         prepare(2)
 
         last = ROUNDS - 1
@@ -273,11 +277,11 @@ def tile_conv2dlinalgrmsnorm_t_kernel(tc, hidden_states, conv_w, norm_w, out):
                 passes(k + 1)
             if k < last:
                 squares(k, 0, RT)
+            if k + 2 < ROUNDS:
+                quantise(k + 2)
             if a < ROUNDS:
                 copy_out(a, 0, on_vector(a, 0))
                 copy_out(a, 1, on_vector(a, 1))
-            if k + 2 < ROUNDS:
-                quantise(k + 2)
             if k < last:
                 rstd(k, 0, RT)
         for j0, j1 in [(0, 2), (2, 4)]:

@@ -137,6 +137,7 @@ def tile_conv2dlinalgrmsnorm_t_kernel(tc, hidden_states, conv_w, norm_w, out):
         code_of = {}
         y_of = {}
         stat_of = {}
+        mom_of = {}
 
         def transposes(k, b):
             xt = psum_x.tile([P, 2, 2, P], F32, tag="xt")
@@ -200,6 +201,23 @@ def tile_conv2dlinalgrmsnorm_t_kernel(tc, hidden_states, conv_w, norm_w, out):
                     accum_out=q[:, j : j + 1],
                 )
 
+        def moments(k):
+            m = stage.tile([P, 8], F32, tag="m")
+            nc.vector.bn_stats(out=m[:, 0:6], in_=y_of[k][1][:].rearrange("p a k -> p k a"))
+            mom_of[k] = m
+
+        def sums(k):
+            m = mom_of[k]
+            q = stat_of[k][0]
+            a = stage.tile([P, 2], F32, tag="a")
+            b = stage.tile([P, 2], F32, tag="b")
+            mean = m[:, 1:7:3]
+            nc.gpsimd.tensor_tensor(out=a[:], in0=mean, in1=mean, op=ALU.mult)
+            nc.gpsimd.tensor_scalar(
+                out=b[:], in0=a[:], scalar1=float(K), scalar2=0.0, op0=ALU.mult, op1=ALU.add
+            )
+            nc.gpsimd.tensor_tensor(out=q[:, 2:4], in0=b[:], in1=m[:, 2:8:3], op=ALU.add)
+
         def rstd(k, j0, j1):
             q, r = stat_of[k]
             nc.scalar.activation(
@@ -232,7 +250,7 @@ def tile_conv2dlinalgrmsnorm_t_kernel(tc, hidden_states, conv_w, norm_w, out):
             )
 
         def on_vector(k, b):
-            return b == 1 or k % 5 == 4
+            return b == 1 and k < 3
 
         def prepare(k):
             for b in range(2):
@@ -267,6 +285,12 @@ def tile_conv2dlinalgrmsnorm_t_kernel(tc, hidden_states, conv_w, norm_w, out):
             if a < ROUNDS:
                 transposes(a, 0)
                 transposes(a, 1)
+            if k + 3 < ROUNDS:
+                squares(k, 0, 2)
+                moments(k)
+                sums(k)
+            elif k < last:
+                squares(k, 0, RT)
             if k >= 1:
                 final(k - 1, 0, RT)
                 if k - 1 >= ROUNDS - 2:
@@ -275,8 +299,6 @@ def tile_conv2dlinalgrmsnorm_t_kernel(tc, hidden_states, conv_w, norm_w, out):
                     store(k - 2, 0, 2 * RT)
             if k + 1 < ROUNDS:
                 passes(k + 1)
-            if k < last:
-                squares(k, 0, RT)
             if k + 2 < ROUNDS:
                 quantise(k + 2)
             if a < ROUNDS:

@@ -27,7 +27,8 @@ PAD = 32
 
 FLOPS = 2 * TOKENS * H * K
 
-W_CHUNKS = [(0, 2), (2, 4), (4, 6), (6, 7), (7, 8)]
+W_LOADS = [(0, 0, 8), (1, 0, 8), (2, 0, 8), (3, 0, 8), (4, 0, 4), (4, 4, 8)]
+W_BANKS = [(0, 2), (2, 4), (4, 6), (6, 8)]
 X_CHUNKS = [(0, 4), (4, 8), (8, 12), (12, 16), (16, 24), (24, 32), (32, 40), (40, 48), (48, 56), (56, 64)]
 
 
@@ -35,7 +36,7 @@ def tile_conv2dlinalgrmsnorm_t_kernel(tc, hidden_states, conv_w, norm_w, out):
     nc = tc.nc
     xv = hidden_states.flatten_outer_dims().rearrange("(n p t) h -> n p (t h)", p=P, t=CT)
     ov = out.flatten_outer_dims().rearrange("(n p t) k -> n p (t k)", p=P, t=CT)
-    wv = conv_w.flatten_outer_dims().rearrange("(i p g) h -> p i g h", i=5, p=P, g=8)
+    wv = conv_w.flatten_outer_dims().rearrange("(i p g) h -> i p (g h)", i=5, p=P, g=8)
 
     with ExitStack() as ctx:
         keep = ctx.enter_context(tc.tile_pool(name="keep", bufs=1))
@@ -46,8 +47,8 @@ def tile_conv2dlinalgrmsnorm_t_kernel(tc, hidden_states, conv_w, norm_w, out):
         ctx.enter_context(tc.manual_schedule())
 
         w_tiles = []
-        for c, (g0, g1) in enumerate(W_CHUNKS):
-            wc = keep.tile([P, 5 * (g1 - g0) * H + PAD], BF16, name=f"wc{c}")
+        for c, (i, g0, g1) in enumerate(W_LOADS):
+            wc = keep.tile([P, (g1 - g0) * H + PAD], BF16, name=f"wc{c}")
             w_tiles.append(wc)
         x_tiles = []
         for c, (t0, t1) in enumerate(X_CHUNKS):
@@ -71,11 +72,10 @@ def tile_conv2dlinalgrmsnorm_t_kernel(tc, hidden_states, conv_w, norm_w, out):
         nc.vector.memset(epsb[:], EPS * H)
         nc.vector.memset(ones[:], 1.0)
         def load_w(c):
-            g0, g1 = W_CHUNKS[c]
-            n = g1 - g0
+            i, g0, g1 = W_LOADS[c]
             nc.sync.dma_start(
-                out=w_tiles[c][:, 0 : 5 * n * H].rearrange("p (i g h) -> p i g h", i=5, g=n),
-                in_=wv[:, :, g0:g1, :],
+                out=w_tiles[c][:, 0 : (g1 - g0) * H],
+                in_=wv[i][:, g0 * H : g1 * H],
             )
 
         def load_x(c):
@@ -90,9 +90,10 @@ def tile_conv2dlinalgrmsnorm_t_kernel(tc, hidden_states, conv_w, norm_w, out):
         nc.sync.dma_start(out=nwz[0:1, :], in_=norm_w.unsqueeze(0))
         load_w(1)
         load_w(2)
-        load_x(0)
         load_w(3)
+        load_x(0)
         load_w(4)
+        load_w(5)
         for c in range(1, len(X_CHUNKS)):
             load_x(c)
         nc.scalar.activation(out=warm[:], in_=epsb[:], func=ACT.Abs_reciprocal_sqrt)
@@ -106,30 +107,30 @@ def tile_conv2dlinalgrmsnorm_t_kernel(tc, hidden_states, conv_w, norm_w, out):
         nc.vector.tensor_copy(out=sel[:], in_=sel_f[:])
 
         wg4 = wg[:].rearrange("p (j g t) -> p j g t", j=32, g=8, t=4)
-        wt_of = {}
+        w_ps = []
+        for g0, g1 in W_BANKS:
+            wt = psum_y.tile([P, 4, 32 * (g1 - g0)], F32, tag="y")
+            w_ps.append(wt)
 
         def w_sum(c):
-            g0, g1 = W_CHUNKS[c]
-            n = g1 - g0
-            wt = psum_y.tile([P, 4, 32 * n], F32, tag="y")
-            wt_of[c] = wt
-            for g in range(n):
-                for t in range(4):
-                    for i in range(5):
-                        h0 = (i * n + g) * H
+            i, l0, l1 = W_LOADS[c]
+            for wt, (g0, g1) in zip(w_ps, W_BANKS):
+                for g in range(max(g0, l0), min(g1, l1)):
+                    for t in range(4):
+                        h0 = (g - l0) * H
                         nc.tensor.matmul(
-                            out=wt[:, t, 32 * g : 32 * g + 32],
+                            out=wt[:, t, 32 * (g - g0) : 32 * (g - g0) + 32],
                             lhsT=w_tiles[c][:, h0 + t : h0 + H : 4],
                             rhs=sel[:],
-                            start=(i == 0),
-                            stop=(i == 4),
+                            start=(i == 0 and g == g0 and t == 0),
+                            stop=(i == 4 and g == g1 - 1 and t == 3),
                         )
 
-        def w_round(c):
-            g0, g1 = W_CHUNKS[c]
+        def w_round(b):
+            g0, g1 = W_BANKS[b]
             nc.vector.tensor_copy(
                 out=wg4[:, :, g0:g1, :],
-                in_=wt_of[c][:].rearrange("p t (g j) -> p j g t", g=g1 - g0, j=32),
+                in_=w_ps[b][:].rearrange("p t (g j) -> p j g t", g=g1 - g0, j=32),
             )
 
         xt_of = {}
@@ -262,17 +263,16 @@ def tile_conv2dlinalgrmsnorm_t_kernel(tc, hidden_states, conv_w, norm_w, out):
         nw_ps = psum_x.tile([P, K], F32, tag="xt")
         nc.tensor.matmul(out=nw_ps[:], lhsT=ones[:], rhs=nwz[:], start=True, stop=True)
         nc.vector.tensor_scalar_mul(out=nwp[:], in0=nw_ps[:], scalar1=math.sqrt(H) / LAYERS)
-        w_round(0)
-        w_sum(1)
-        w_round(1)
-        w_sum(2)
-        w_round(2)
+        for c in range(1, 4):
+            w_sum(c)
         prepare(0)
-        w_sum(3)
-        w_round(3)
         quantise(0)
         w_sum(4)
-        w_round(4)
+        w_round(0)
+        w_round(1)
+        w_sum(5)
+        w_round(2)
+        w_round(3)
         nc.vector.quantize_mx(out=w_codes[:].bitcast(FP8X4), scales=w_scales[:], in_=wg[:])
         prepare(1)
         quantise(1)

@@ -94,7 +94,8 @@ def tile_conv2dlinalgrmsnorm_t_kernel(tc, hidden_states, conv_w, norm_w, out):
         load_x(0)
         load_w(4)
         load_w(5)
-        for c in range(1, len(X_CHUNKS)):
+        load_x(1)
+        for c in range(2, len(X_CHUNKS)):
             load_x(c)
         nc.scalar.activation(out=warm[:], in_=epsb[:], func=ACT.Abs_reciprocal_sqrt)
         make_identity(nc, ident[:])
@@ -126,12 +127,14 @@ def tile_conv2dlinalgrmsnorm_t_kernel(tc, hidden_states, conv_w, norm_w, out):
                             stop=(i == 4 and g == g1 - 1 and t == 3),
                         )
 
-        def w_round(b):
+        def w_round(b, on_vector):
             g0, g1 = W_BANKS[b]
-            nc.vector.tensor_copy(
-                out=wg4[:, :, g0:g1, :],
-                in_=w_ps[b][:].rearrange("p t (g j) -> p j g t", g=g1 - g0, j=32),
-            )
+            dst = wg4[:, :, g0:g1, :]
+            src = w_ps[b][:].rearrange("p t (g j) -> p j g t", g=g1 - g0, j=32)
+            if on_vector:
+                nc.vector.tensor_copy(out=dst, in_=src)
+            else:
+                nc.scalar.copy(out=dst, in_=src)
 
         xt_of = {}
         grp_of = {}
@@ -251,7 +254,10 @@ def tile_conv2dlinalgrmsnorm_t_kernel(tc, hidden_states, conv_w, norm_w, out):
             )
 
         def on_vector(k, b):
-            return b == 1 and k < 3
+            return b == 1 and k < 2
+
+        def all_on_scalar(k):
+            return k in (ROUNDS // 2, ROUNDS - 3)
 
         def prepare(k):
             for b in range(2):
@@ -268,15 +274,18 @@ def tile_conv2dlinalgrmsnorm_t_kernel(tc, hidden_states, conv_w, norm_w, out):
         prepare(0)
         quantise(0)
         w_sum(4)
-        w_round(0)
-        w_round(1)
+        w_round(0, True)
+        w_round(1, False)
         w_sum(5)
-        w_round(2)
-        w_round(3)
+        w_round(2, True)
+        w_round(3, False)
         nc.vector.quantize_mx(out=w_codes[:].bitcast(FP8X4), scales=w_scales[:], in_=wg[:])
         prepare(1)
-        quantise(1)
         passes(0)
+        squares(0, 0, 2)
+        moments(0)
+        sums(0)
+        quantise(1)
         prepare(2)
 
         last = ROUNDS - 1
@@ -285,18 +294,15 @@ def tile_conv2dlinalgrmsnorm_t_kernel(tc, hidden_states, conv_w, norm_w, out):
             if a < ROUNDS:
                 transposes(a, 0)
                 transposes(a, 1)
-            if k + 3 < ROUNDS:
+            if all_on_scalar(k):
+                squares(k, 0, RT)
+            elif 0 < k < last:
                 squares(k, 0, 2)
                 moments(k)
                 sums(k)
-            elif k < last:
-                squares(k, 0, RT)
             if k >= 1:
                 final(k - 1, 0, RT)
-                if k - 1 >= ROUNDS - 2:
-                    store(k - 1, 0, RT)
-                elif (k - 1) % 2 == 1:
-                    store(k - 2, 0, 2 * RT)
+                store(k - 1, 0, RT)
             if k + 1 < ROUNDS:
                 passes(k + 1)
             if k + 2 < ROUNDS:

@@ -41,6 +41,7 @@ def tile_conv2dlinalgrmsnorm_t_kernel(tc, hidden_states, conv_w, norm_w, out):
     with ExitStack() as ctx:
         keep = ctx.enter_context(tc.tile_pool(name="keep", bufs=1))
         stage = ctx.enter_context(tc.tile_pool(name="stage", bufs=3))
+        junks = ctx.enter_context(tc.tile_pool(name="junks", bufs=8))
         codes = ctx.enter_context(tc.tile_pool(name="codes", bufs=4))
         psum_x = ctx.enter_context(tc.psum_pool(name="psum_x", bufs=3))
         psum_y = ctx.enter_context(tc.psum_pool(name="psum_y", bufs=5))
@@ -63,7 +64,6 @@ def tile_conv2dlinalgrmsnorm_t_kernel(tc, hidden_states, conv_w, norm_w, out):
         nwp = keep.tile([P, K], F32)
         epsb = keep.tile([P, 1], F32)
         warm = keep.tile([P, 1], F32)
-        junk = keep.tile([P, K], BF16)
         wg = keep.tile([P, 4 * K], BF16, align_bytes=64)
         w_codes = keep.tile([P, K], U32, align_bytes=64)
         w_scales = keep.tile([P, K], U8, align_bytes=64)
@@ -198,6 +198,7 @@ def tile_conv2dlinalgrmsnorm_t_kernel(tc, hidden_states, conv_w, norm_w, out):
                 stat_of[k] = (q, r)
             q = stat_of[k][0]
             for j in range(j0, j1):
+                junk = junks.tile([P, K], BF16, tag="junk")
                 nc.scalar.activation(
                     out=junk[:],
                     in_=y_of[k][j // 2][:, j % 2, :],

@@ -258,7 +258,7 @@ def tile_conv2dlinalgrmsnorm_t_kernel(tc, hidden_states, conv_w, norm_w, out):
             return b == 1 and k < 2
 
         def all_on_scalar(k):
-            return k in (ROUNDS // 2, ROUNDS - 3)
+            return k in (5, 9, 13, 14)
 
         def prepare(k):
             for b in range(2):

@@ -203,6 +203,7 @@ def tile_conv2dlinalgrmsnorm_t_kernel(tc, hidden_states, conv_w, norm_w, out):
                     out=junk[:],
                     in_=y_of[k][j // 2][:, j % 2, :],
                     func=ACT.Square,
+                    scale=1.0 / 16,
                     accum_out=q[:, j : j + 1],
                 )
 
@@ -217,11 +218,11 @@ def tile_conv2dlinalgrmsnorm_t_kernel(tc, hidden_states, conv_w, norm_w, out):
             a = stage.tile([P, 2], F32, tag="a")
             b = stage.tile([P, 2], F32, tag="b")
             mean = m[:, 1:7:3]
-            nc.gpsimd.tensor_tensor(out=a[:], in0=mean, in1=mean, op=ALU.mult)
             nc.gpsimd.tensor_scalar(
-                out=b[:], in0=a[:], scalar1=float(K), scalar2=0.0, op0=ALU.mult, op1=ALU.add
+                out=b[:], in0=m[:, 2:8:3], scalar1=1.0 / K, scalar2=0.0, op0=ALU.mult, op1=ALU.add
             )
-            nc.gpsimd.tensor_tensor(out=q[:, 2:4], in0=b[:], in1=m[:, 2:8:3], op=ALU.add)
+            nc.gpsimd.tensor_tensor(out=a[:], in0=mean, in1=mean, op=ALU.mult)
+            nc.gpsimd.tensor_tensor(out=q[:, 2:4], in0=a[:], in1=b[:], op=ALU.add)
 
         def rstd(k, j0, j1):
             q, r = stat_of[k]
@@ -230,7 +231,7 @@ def tile_conv2dlinalgrmsnorm_t_kernel(tc, hidden_states, conv_w, norm_w, out):
                 in_=q[:, j0:j1],
                 func=ACT.Abs_reciprocal_sqrt,
                 bias=epsb[:],
-                scale=1.0 / (LAYERS * LAYERS),
+                scale=K / (LAYERS * LAYERS),
             )
 
         def final(k, j0, j1):
@@ -258,7 +259,7 @@ def tile_conv2dlinalgrmsnorm_t_kernel(tc, hidden_states, conv_w, norm_w, out):
             return b == 1 and k < 2
 
         def all_on_scalar(k):
-            return k in (5, 9, 13, 14)
+            return k % 3 == 2 or k == ROUNDS - 3
 
         def prepare(k):
             for b in range(2):

@@ -259,7 +259,7 @@ def tile_conv2dlinalgrmsnorm_t_kernel(tc, hidden_states, conv_w, norm_w, out):
             return b == 1 and k < 2
 
         def all_on_scalar(k):
-            return k % 3 == 2 or k == ROUNDS - 3
+            return 1 < k < last and k % 2 == 1 or k == ROUNDS - 2
 
         def prepare(k):
             for b in range(2):
@@ -287,8 +287,10 @@ def tile_conv2dlinalgrmsnorm_t_kernel(tc, hidden_states, conv_w, norm_w, out):
         squares(0, 0, 2)
         moments(0)
         sums(0)
+        rstd(0, 0, 2)
         quantise(1)
         prepare(2)
+        final(0, 0, 2)
 
         last = ROUNDS - 1
         for k in range(ROUNDS):
@@ -296,14 +298,17 @@ def tile_conv2dlinalgrmsnorm_t_kernel(tc, hidden_states, conv_w, norm_w, out):
             if a < ROUNDS:
                 transposes(a, 0)
                 transposes(a, 1)
-            if all_on_scalar(k):
-                squares(k, 0, RT)
-            elif 0 < k < last:
+            if 0 < k < last:
                 squares(k, 0, 2)
+            if k >= 1 and not all_on_scalar(k - 1):
+                rstd(k - 1, 2, RT)
+            if all_on_scalar(k):
+                squares(k, 2, RT)
+            elif 0 < k < last:
                 moments(k)
                 sums(k)
             if k >= 1:
-                final(k - 1, 0, RT)
+                final(k - 1, 2 if k == 1 else 0, RT)
                 store(k - 1, 0, RT)
             if k + 1 < ROUNDS:
                 passes(k + 1)
@@ -312,8 +317,8 @@ def tile_conv2dlinalgrmsnorm_t_kernel(tc, hidden_states, conv_w, norm_w, out):
             if a < ROUNDS:
                 copy_out(a, 0, on_vector(a, 0))
                 copy_out(a, 1, on_vector(a, 1))
-            if k < last:
-                rstd(k, 0, RT)
+            if 0 < k < last:
+                rstd(k, 0, RT if all_on_scalar(k) else 2)
         for j0, j1 in [(0, 2), (2, 4)]:
             squares(last, j0, j1)
             rstd(last, j0, j1)

import math
from contextlib import ExitStack

import concourse.mybir as mybir
from concourse.masks import make_identity

F32 = mybir.dt.float32
BF16 = mybir.dt.bfloat16
U32 = mybir.dt.uint32
U8 = mybir.dt.uint8
FP8X4 = mybir.dt.float8_e4m3fn_x4
ALU = mybir.AluOpType
ACT = mybir.ActivationFunctionType

P = 128
TOKENS = 8192
H = 512
K = 256
LAYERS = 20
EPS = 1e-06
TILES = TOKENS // P
CT = 8
RT = 4
ROUNDS = TILES // RT

PAD = 32

FLOPS = 2 * TOKENS * H * K

W_LOADS = [(0, 0, 8), (1, 0, 8), (2, 0, 8), (3, 0, 8), (4, 0, 4), (4, 4, 8)]
W_BANKS = [(0, 2), (2, 4), (4, 6), (6, 8)]
X_CHUNKS = [(0, 4), (4, 8), (8, 12), (12, 16), (16, 24), (24, 32), (32, 40), (40, 48), (48, 56), (56, 64)]


def tile_conv2dlinalgrmsnorm_t_kernel(tc, hidden_states, conv_w, norm_w, out):
    nc = tc.nc
    xv = hidden_states.flatten_outer_dims().rearrange("(n p t) h -> n p (t h)", p=P, t=CT)
    ov = out.flatten_outer_dims().rearrange("(n p t) k -> n p (t k)", p=P, t=CT)
    wv = conv_w.flatten_outer_dims().rearrange("(i p g) h -> i p (g h)", i=5, p=P, g=8)

    with ExitStack() as ctx:
        keep = ctx.enter_context(tc.tile_pool(name="keep", bufs=1))
        stage = ctx.enter_context(tc.tile_pool(name="stage", bufs=3))
        junks = ctx.enter_context(tc.tile_pool(name="junks", bufs=8))
        codes = ctx.enter_context(tc.tile_pool(name="codes", bufs=4))
        psum_x = ctx.enter_context(tc.psum_pool(name="psum_x", bufs=3))
        psum_y = ctx.enter_context(tc.psum_pool(name="psum_y", bufs=5))
        ctx.enter_context(tc.manual_schedule())

        w_tiles = []
        for c, (i, g0, g1) in enumerate(W_LOADS):
            wc = keep.tile([P, (g1 - g0) * H + PAD], BF16, name=f"wc{c}")
            w_tiles.append(wc)
        x_tiles = []
        for c, (t0, t1) in enumerate(X_CHUNKS):
            xc = keep.tile([P, (t1 - t0) * H + PAD], BF16, name=f"xc{c}")
            x_tiles.append(xc)
        out_sb = keep.tile([P, TILES * K], F32)
        ident = keep.tile([P, P], F32)
        sel_f = keep.tile([P, 32], F32)
        sel = keep.tile([P, 32], BF16)
        ones = keep.tile([P, P], BF16)
        nwz = keep.tile([P, K], BF16)
        nwp = keep.tile([P, K], F32)
        epsb = keep.tile([P, 1], F32)
        warm = keep.tile([P, 1], F32)
        wg = keep.tile([P, 4 * K], BF16, align_bytes=64)
        w_codes = keep.tile([P, K], U32, align_bytes=64)
        w_scales = keep.tile([P, K], U8, align_bytes=64)

        nc.vector.memset(nwz[:], 0.0)
        nc.vector.memset(epsb[:], EPS * H)
        nc.vector.memset(ones[:], 1.0)
        def load_w(c):
            i, g0, g1 = W_LOADS[c]
            nc.sync.dma_start(
                out=w_tiles[c][:, 0 : (g1 - g0) * H],
                in_=wv[i][:, g0 * H : g1 * H],
            )

        def load_x(c):
            t0, t1 = X_CHUNKS[c]
            n, u0 = divmod(t0, CT)
            nc.sync.dma_start(
                out=x_tiles[c][:, 0 : (t1 - t0) * H],
                in_=xv[n][:, u0 * H : (u0 + t1 - t0) * H],
            )

        load_w(0)
        nc.sync.dma_start(out=nwz[0:1, :], in_=norm_w.unsqueeze(0))
        load_w(1)
        load_w(2)
        load_w(3)
        load_x(0)
        load_w(4)
        load_w(5)
        load_x(1)
        for c in range(2, len(X_CHUNKS)):
            load_x(c)
        nc.scalar.activation(out=warm[:], in_=epsb[:], func=ACT.Abs_reciprocal_sqrt)
        make_identity(nc, ident[:])
        nc.vector.tensor_reduce(
            out=sel_f[:],
            in_=ident[:].rearrange("p (a n) -> p n a", a=4),
            axis=mybir.AxisListType.X,
            op=ALU.add,
        )
        nc.vector.tensor_copy(out=sel[:], in_=sel_f[:])

        wg4 = wg[:].rearrange("p (j g t) -> p j g t", j=32, g=8, t=4)
        w_ps = []
        for g0, g1 in W_BANKS:
            wt = psum_y.tile([P, 4, 32 * (g1 - g0)], F32, tag="y")
            w_ps.append(wt)

        def w_sum(c):
            i, l0, l1 = W_LOADS[c]
            for wt, (g0, g1) in zip(w_ps, W_BANKS):
                for g in range(max(g0, l0), min(g1, l1)):
                    for t in range(4):
                        h0 = (g - l0) * H
                        nc.tensor.matmul(
                            out=wt[:, t, 32 * (g - g0) : 32 * (g - g0) + 32],
                            lhsT=w_tiles[c][:, h0 + t : h0 + H : 4],
                            rhs=sel[:],
                            start=(i == 0 and g == g0 and t == 0),
                            stop=(i == 4 and g == g1 - 1 and t == 3),
                        )

        def w_round(b, on_vector):
            g0, g1 = W_BANKS[b]
            dst = wg4[:, :, g0:g1, :]
            src = w_ps[b][:].rearrange("p t (g j) -> p j g t", g=g1 - g0, j=32)
            if on_vector:
                nc.vector.tensor_copy(out=dst, in_=src)
            else:
                nc.scalar.copy(out=dst, in_=src)

        xt_of = {}
        grp_of = {}
        code_of = {}
        y_of = {}
        stat_of = {}
        mom_of = {}

        def transposes(k, b):
            xt = psum_x.tile([P, 2, 2, P], F32, tag="xt")
            for a in range(2):
                t = RT * k + 2 * b + a
                c = [i for i, (t0, t1) in enumerate(X_CHUNKS) if t0 <= t < t1][0]
                xw = x_tiles[c][:].bitcast(F32)
                c0 = 256 * (t - X_CHUNKS[c][0])
                for u in range(2):
                    nc.tensor.transpose(xt[:, a, u, :], xw[:, c0 + u : c0 + 256 : 2], ident[:])
            xt_of[(k, b)] = xt

        def copy_out(k, b, on_vector):
            if b == 0:
                grp = stage.tile([P, RT * H], BF16, align_bytes=64, tag="grp")
                grp_of[k] = grp
            g32 = grp_of[k][:].bitcast(F32)
            dst = g32[:, 512 * b : 512 * b + 512].rearrange("p (a r u) -> p a r u", a=2, r=P, u=2)
            src = xt_of[(k, b)][:].rearrange("p a u r -> p a r u")
            if on_vector:
                nc.vector.tensor_copy(out=dst, in_=src)
            else:
                nc.scalar.copy(out=dst, in_=src)

        def quantise(k):
            xc = codes.tile([P, RT * P], U32, align_bytes=64, tag="xc")
            xs = codes.tile([P, RT * P], U8, align_bytes=64, tag="xs")
            nc.vector.quantize_mx(out=xc[:].bitcast(FP8X4), scales=xs[:], in_=grp_of[k][:])
            code_of[k] = (xc, xs)

        def passes(k):
            xc, xs = code_of[k]
            banks = []
            for b in range(2):
                y = psum_y.tile([P, 2, K], F32, tag="y")
                for a in range(2):
                    c0 = P * (2 * b + a)
                    nc.tensor.matmul_mx(
                        out=y[:, a, :],
                        lhsT=xc[:, c0 : c0 + P].bitcast(FP8X4),
                        lhsT_scale=xs[:, c0 : c0 + P],
                        rhs=w_codes[:].bitcast(FP8X4),
                        rhs_scale=w_scales[:],
                        start=True,
                        stop=True,
                    )
                banks.append(y)
            y_of[k] = banks

        def squares(k, j0, j1):
            if j0 == 0:
                q = stage.tile([P, RT], F32, tag="q")
                r = stage.tile([P, RT], F32, tag="r")
                stat_of[k] = (q, r)
            q = stat_of[k][0]
            for j in range(j0, j1):
                junk = junks.tile([P, K], BF16, tag="junk")
                nc.scalar.activation(
                    out=junk[:],
                    in_=y_of[k][j // 2][:, j % 2, :],
                    func=ACT.Square,
                    scale=1.0 / 16,
                    accum_out=q[:, j : j + 1],
                )

        def moments(k):
            m = stage.tile([P, 8], F32, tag="m")
            nc.vector.bn_stats(out=m[:, 0:6], in_=y_of[k][1][:].rearrange("p a k -> p k a"))
            mom_of[k] = m

        def sums(k):
            m = mom_of[k]
            q = stat_of[k][0]
            a = stage.tile([P, 2], F32, tag="a")
            b = stage.tile([P, 2], F32, tag="b")
            mean = m[:, 1:7:3]
            nc.gpsimd.tensor_scalar(
                out=b[:], in0=m[:, 2:8:3], scalar1=1.0 / K, scalar2=0.0, op0=ALU.mult, op1=ALU.add
            )
            nc.gpsimd.tensor_tensor(out=a[:], in0=mean, in1=mean, op=ALU.mult)
            nc.gpsimd.tensor_tensor(out=q[:, 2:4], in0=a[:], in1=b[:], op=ALU.add)

        def rstd(k, j0, j1):
            q, r = stat_of[k]
            nc.scalar.activation(
                out=r[:, j0:j1],
                in_=q[:, j0:j1],
                func=ACT.Abs_reciprocal_sqrt,
                bias=epsb[:],
                scale=K / (LAYERS * LAYERS),
            )

        def final(k, j0, j1):
            r = stat_of[k][1]
            for j in range(j0, j1):
                t = RT * k + j
                nc.vector.scalar_tensor_tensor(
                    out=out_sb[:, t * K : (t + 1) * K],
                    in0=y_of[k][j // 2][:, j % 2, :],
                    scalar=r[:, j : j + 1],
                    in1=nwp[:],
                    op0=ALU.mult,
                    op1=ALU.mult,
                )

        def store(k, j0, j1):
            t0 = RT * k + j0
            t1 = RT * k + j1
            n, u0 = divmod(t0, CT)
            nc.sync.dma_start(
                out=ov[n][:, u0 * K : (u0 + t1 - t0) * K], in_=out_sb[:, t0 * K : t1 * K]
            )

        def on_vector(k, b):
            return b == 1 and k < 2

        def all_on_scalar(k):
            return 1 < k < last and k % 2 == 1 or k == ROUNDS - 2

        def prepare(k):
            for b in range(2):
                transposes(k, b)
            for b in range(2):
                copy_out(k, b, on_vector(k, b))

        w_sum(0)
        nw_ps = psum_x.tile([P, K], F32, tag="xt")
        nc.tensor.matmul(out=nw_ps[:], lhsT=ones[:], rhs=nwz[:], start=True, stop=True)
        nc.vector.tensor_scalar_mul(out=nwp[:], in0=nw_ps[:], scalar1=math.sqrt(H) / LAYERS)
        for c in range(1, 4):
            w_sum(c)
        prepare(0)
        quantise(0)
        w_sum(4)
        w_round(0, True)
        w_round(1, False)
        w_sum(5)
        w_round(2, True)
        w_round(3, False)
        nc.vector.quantize_mx(out=w_codes[:].bitcast(FP8X4), scales=w_scales[:], in_=wg[:])
        prepare(1)
        passes(0)
        squares(0, 0, 2)
        moments(0)
        sums(0)
        rstd(0, 0, 2)
        quantise(1)
        prepare(2)
        final(0, 0, 2)

        last = ROUNDS - 1
        for k in range(ROUNDS):
            a = k + 3
            if a < ROUNDS:
                transposes(a, 0)
                transposes(a, 1)
            if 0 < k < last:
                squares(k, 0, 2)
            if k >= 1 and not all_on_scalar(k - 1):
                rstd(k - 1, 2, RT)
            if all_on_scalar(k):
                squares(k, 2, RT)
            elif 0 < k < last:
                moments(k)
                sums(k)
            if k >= 1:
                final(k - 1, 2 if k == 1 else 0, RT)
                store(k - 1, 0, RT)
            if k + 1 < ROUNDS:
                passes(k + 1)
            if k + 2 < ROUNDS:
                quantise(k + 2)
            if a < ROUNDS:
                copy_out(a, 0, on_vector(a, 0))
                copy_out(a, 1, on_vector(a, 1))
            if 0 < k < last:
                rstd(k, 0, RT if all_on_scalar(k) else 2)
        for j0, j1 in [(0, 2), (2, 4)]:
            squares(last, j0, j1)
            rstd(last, j0, j1)
            for j in range(j0, j1):
                final(last, j, j + 1)
                store(last, j, j + 1)
